import numpy as np
import ml_dtypes


def mxq(x, axis, fmt="e4m3"):
    dtype, down = {"e4m3": (ml_dtypes.float8_e4m3fn, 7), "e5m2": (ml_dtypes.float8_e5m2, 14)}[fmt]
    v = np.moveaxis(np.asarray(x, np.float32).astype(ml_dtypes.bfloat16).astype(np.float64), axis, -1)
    blocks = v.reshape(v.shape[:-1] + (-1, 32))
    amax = np.abs(blocks).max(-1, keepdims=True)
    byte = np.maximum(np.where(amax > 0, np.frexp(amax)[1] - 1 + 127, 0) - down, 1)
    scale = np.exp2(byte - 127.0)
    codes = (blocks / scale).astype(np.float32).astype(dtype).astype(np.float64)
    return np.moveaxis((codes * scale).reshape(v.shape), -1, axis)


WIDE = False


def mx_kscale(k):
    if not WIDE:
        return np.ones(k)
    levels = np.array([10, -10, 5, -5, 0])
    if k % 512:
        return np.exp2(np.random.permutation(np.resize(levels, k // 32))).repeat(32)
    a = np.empty((k // 512, 16))
    for p in range(k // 512):
        a[p, :8] = np.random.permutation(np.resize(levels, 8))
        for g in range(8):
            far = levels[np.abs(levels - a[p, g]) >= 10]
            a[p, g + 8] = far[np.random.randint(len(far))]
    return np.exp2(a.ravel()).repeat(32)


BF16 = ml_dtypes.bfloat16


def bf(x):
    return np.asarray(x, np.float32).astype(BF16)


def f64(x):
    return np.asarray(x).astype(np.float64)


IN, H, C, B = 1024, 1024, 2, 512
QH = H % 512 == 0


def sigmoid(v):
    return 1.0 / (1.0 + np.exp(-v))


def draw0():
    s = mx_kscale(IN)
    t = mx_kscale(H) if QH else np.ones(H)
    return {"input_word": bf(np.random.standard_normal((B, IN)) * s),
            "hidden_states": bf(np.random.standard_normal((B, H)) * t),
            "Wx": bf(np.random.uniform(-1.0, 1.0, (C, 2 * H, IN)) / np.sqrt(IN) / s),
            "bx": bf(np.random.standard_normal((C, 2 * H)) * 0.3),
            "Wh": bf(np.random.uniform(-1.0, 1.0, (C, 2 * H, H)) / np.sqrt(H) / t)}


def core(input_word, hidden_states, Wx, bx, Wh):
    px = mxq(f64(input_word), 1, "e4m3") @ mxq(f64(Wx), 2, "e4m3").transpose(0, 2, 1)
    if QH:
        ph = mxq(f64(hidden_states), 1, "e4m3") @ mxq(f64(Wh), 2, "e4m3").transpose(0, 2, 1)
    else:
        ph = f64(hidden_states) @ f64(Wh).transpose(0, 2, 1)
    net = px.transpose(1, 0, 2) + ph.transpose(1, 0, 2) + f64(bx)[None, :, :]
    input_gate, cell_states = net[..., :H], net[..., H:]
    cell_input = np.tanh(cell_states)
    input_gate = sigmoid(input_gate)
    return (cell_input, input_gate)


def e4m3fn_bytes(y):
    return np.clip(np.asarray(y, np.float64), -448.0, 448.0).astype(np.float32).astype(ml_dtypes.float8_e4m3fn).view(np.uint8)


def e4m3fn_values(b):
    return np.asarray(b, np.uint8).view(ml_dtypes.float8_e4m3fn).astype(np.float64)


def setup_inputs():
    d = draw0()
    x0 = np.asarray(d['Wx']).astype(np.float64)
    s = (np.max(np.abs(x0), axis=(0, 1), keepdims=True) / 448.0).astype(np.float32)
    out = {}
    for k, v in d.items():
        if k == 'Wx':
            out['Wx_bytes'] = e4m3fn_bytes(x0 / s.astype(np.float64))
            out['Wx_scale'] = s
        else:
            out[k] = v
    return out


def reference(input_word, hidden_states, Wx_bytes, Wx_scale, bx, Wh):
    return core(input_word, hidden_states, e4m3fn_values(Wx_bytes) * Wx_scale.astype(np.float64), bx, Wh)

@@ -1,0 +1,263 @@
+from contextlib import ExitStack
+
+import concourse.mybir as mybir
+from concourse.masks import make_identity
+
+F32 = mybir.dt.float32
+BF16 = mybir.dt.bfloat16
+U32 = mybir.dt.uint32
+U8 = mybir.dt.uint8
+FP8 = mybir.dt.float8_e4m3fn
+FP8X4 = mybir.dt.float8_e4m3fn_x4
+ACT = mybir.ActivationFunctionType
+ALU = mybir.AluOpType
+
+P = 128
+B = 512
+K = 1024
+H = 1024
+C = 2
+NCH = 512
+FLOPS = 2 * B * (C * 2 * H) * (2 * K)
+LAG = 5
+
+
+def tile_compute_gate_kernel(tc, input_word, hidden_states, Wx_bytes, Wx_scale, bx, Wh, out_0, out_1):
+    nc = tc.nc
+
+    chunks = []
+    for c in range(C):
+        for hf in range(2):
+            chunks.append((c, hf * NCH, ACT.Sigmoid, out_1, hf * NCH))
+    for c in range(C):
+        for hf in range(2):
+            chunks.append((c, H + hf * NCH, ACT.Tanh, out_0, hf * NCH))
+    n_chunks = len(chunks)
+
+    with ExitStack() as ctx:
+        const = ctx.enter_context(tc.tile_pool(name="const", bufs=1))
+        raw = ctx.enter_context(tc.tile_pool(name="raw", bufs=1))
+        wide = ctx.enter_context(tc.tile_pool(name="wide", bufs=3))
+        grpp = ctx.enter_context(tc.tile_pool(name="grpp", bufs=4))
+        codep = ctx.enter_context(tc.tile_pool(name="codep", bufs=3))
+        outp = ctx.enter_context(tc.tile_pool(name="outp", bufs=6))
+        psum = ctx.enter_context(tc.psum_pool(name="psum", bufs=1))
+        ctx.enter_context(tc.manual_schedule())
+
+        scale2 = const.tile([P, 2, K], F32, name="scale2")
+        nc.scalar.dma_start(out=scale2[:, 0, :], in_=Wx_scale.rearrange("a b k -> (a b k)").partition_broadcast(P))
+
+        wxq = []
+        wh_raw = []
+        for n in range(n_chunks):
+            wxq_n = raw.tile([P, 4, K], U8, name="wxq%d" % n, tag="wxq%d" % n)
+            wxq.append(wxq_n)
+            wh_n = raw.tile([P, 4, K], BF16, name="whr%d" % n, tag="whr%d" % n)
+            wh_raw.append(wh_n)
+        h_raw = raw.tile([P, 4, K], BF16, name="h_raw")
+        x_raw = raw.tile([P, 4, K], BF16, name="x_raw")
+        bias = const.tile([P, C * 2 * H], BF16, name="bias")
+
+        def load_wx(n, parts):
+            c, j0 = chunks[n][0], chunks[n][1]
+            src = Wx_bytes[c, j0:j0 + NCH, :].rearrange("(p a) k -> p a k", a=4)
+            for i in parts:
+                nc.sync.dma_start(out=wxq[n][:, 2 * i:2 * i + 2, :], in_=src[:, 2 * i:2 * i + 2, :])
+
+        def load_wx_whole(n):
+            c, j0 = chunks[n][0], chunks[n][1]
+            nc.sync.dma_start(out=wxq[n][:], in_=Wx_bytes[c, j0:j0 + NCH, :].rearrange("(p a) k -> p a k", a=4))
+
+        def load_bias(n):
+            c, j0 = chunks[n][0], chunks[n][1]
+            b0 = c * 2 * H + j0
+            nc.sync.dma_start(out=bias[:, b0:b0 + NCH], in_=bx[c, j0:j0 + NCH].partition_broadcast(P))
+
+        def load_wh(n, parts):
+            c, j0 = chunks[n][0], chunks[n][1]
+            src = Wh[c, j0:j0 + NCH, :].rearrange("(p a) k -> p a k", a=4)
+            step = 4 // parts
+            for i in range(parts):
+                nc.sync.dma_start(out=wh_raw[n][:, i * step:(i + 1) * step, :], in_=src[:, i * step:(i + 1) * step, :])
+
+        def load_act(dst, src_ap, a0, a1):
+            src = src_ap.rearrange("(p a) k -> p a k", a=4)
+            nc.sync.dma_start(out=dst[:, a0:a1, :], in_=src[:, a0:a1, :])
+
+        load_act(h_raw, hidden_states, 0, 1)
+        load_wx(0, [0])
+        load_act(h_raw, hidden_states, 1, 2)
+        load_act(h_raw, hidden_states, 2, 4)
+        load_wx(0, [1])
+        load_act(x_raw, input_word, 0, 2)
+        load_act(x_raw, input_word, 2, 4)
+        load_wh(0, 2)
+        load_wx_whole(1)
+        load_wh(1, 1)
+        load_wh(2, 1)
+        load_wx_whole(2)
+        load_bias(0)
+        load_wh(3, 1)
+
+        ident = const.tile([P, P], F32, name="ident")
+        make_identity(nc, ident[:])
+        junk = const.tile([P, 8], F32, name="junk")
+        nc.vector.memset(junk[:], 0.0)
+        nc.scalar.activation(out=junk[:, 0:1], in_=junk[:, 0:1], func=ACT.Sigmoid)
+        nc.scalar.copy(out=scale2[:, 1, :], in_=scale2[:, 0, :])
+
+        a_codes = const.tile([P, 4, B], U32, name="a_codes", align_bytes=64)
+        a_scl = const.tile([P, 4, B], U8, name="a_scl", align_bytes=64)
+
+        wxb = {}
+        w_codes = {}
+        w_scl = {}
+        banks = {}
+        grps = {}
+        accs = {}
+        outs = {}
+
+        def widen(w):
+            n, ap = w // 2, w % 2
+            if ap == 0:
+                wxb_n = wide.tile([P, 4, K], BF16, name="wxb")
+                wxb[n] = wxb_n
+            if w == 0:
+                for a in range(2):
+                    nc.vector.tensor_tensor(out=wxb[n][:, a, :], in0=wxq[n][:, a, :].bitcast(FP8), in1=scale2[:, 0, :], op=ALU.mult)
+            else:
+                nc.vector.tensor_tensor(
+                    out=wxb[n][:, 2 * ap:2 * ap + 2, :].rearrange("p a k -> p (a k)"),
+                    in0=wxq[n][:, 2 * ap:2 * ap + 2, :].rearrange("p a k -> p (a k)").bitcast(FP8),
+                    in1=scale2[:].rearrange("p a k -> p (a k)"),
+                    op=ALU.mult,
+                )
+
+        seq = [("act", h_raw, 0), ("act", x_raw, 2), ("w", 0, 0), ("w", 0, 2), ("w", 1, 0)]
+        for n in range(1, n_chunks - 1):
+            seq.append(("w", n + 1, 0))
+            seq.append(("w", n, 2))
+        seq.append(("w", n_chunks - 1, 2))
+        n_units = len(seq)
+
+        def unit_src(s):
+            kind, what, ps0 = seq[s]
+            if kind == "act":
+                return what
+            return wh_raw[what] if ps0 == 0 else wxb[what]
+
+        def transposes(s):
+            src = unit_src(s)
+            for g in range(2):
+                for ap in range(2):
+                    b = 2 * g + ap
+                    tp = psum.tile([P, 2, 256], F32, name="tp%d" % b, tag="tp%d" % b)
+                    banks[(s, b)] = tp
+                    for al in range(2):
+                        words = src[:, 2 * ap + al, :].bitcast(F32)
+                        for u in range(2):
+                            nc.tensor.transpose(tp[:, u, al * P:(al + 1) * P], words[:, 256 * g + u:256 * (g + 1):2], ident[:])
+
+        def copy_out(s, b):
+            g, ap = b // 2, b % 2
+            if ap == 0:
+                grp = grpp.tile([P, NCH, 4], BF16, name="grp", align_bytes=64)
+                grps[(s, g)] = grp
+            grp = grps[(s, g)]
+            dst = grp[:, ap * 256:(ap + 1) * 256, :].rearrange("p c t -> p (c t)").bitcast(F32).rearrange("p (c u) -> p c u", u=2)
+            nc.scalar.copy(out=dst, in_=banks[(s, b)][:].rearrange("p u c -> p c u"))
+
+        def quant(s, g):
+            kind, what, ps0 = seq[s]
+            if kind == "act":
+                cod, scl = a_codes, a_scl
+            else:
+                if ps0 == 0 and g == 0:
+                    wc = codep.tile([P, 4, NCH], U32, name="wc", align_bytes=64)
+                    ws = codep.tile([P, 4, NCH], U8, name="ws", align_bytes=64)
+                    w_codes[what] = wc
+                    w_scl[what] = ws
+                cod, scl = w_codes[what], w_scl[what]
+            nc.vector.quantize_mx(
+                out=cod[:, ps0 + g, :].bitcast(FP8X4),
+                scales=scl[:, ps0 + g, :],
+                in_=grps[(s, g)][:].rearrange("p c t -> p (c t)"),
+            )
+
+        def matmuls(j):
+            n = j // 2
+            for mi in range(2):
+                m = 2 * (j % 2) + mi
+                acc = psum.tile([P, NCH], F32, name="acc%d" % m, tag="acc%d" % m)
+                accs[(j, mi)] = acc
+                for ps in range(4):
+                    nc.tensor.matmul_mx(
+                        out=acc[:],
+                        lhsT=a_codes[:, ps, m * P:(m + 1) * P].bitcast(FP8X4),
+                        lhsT_scale=a_scl[:, ps, m * P:(m + 1) * P],
+                        rhs=w_codes[n][:, ps, :].bitcast(FP8X4),
+                        rhs_scale=w_scl[n][:, ps, :],
+                        start=(ps == 0),
+                        stop=(ps == 3),
+                    )
+
+        def add_bias(j, mi, r0, r1):
+            c, j0 = chunks[j // 2][0], chunks[j // 2][1]
+            b0 = c * 2 * H + j0
+            if r0 == 0:
+                o = outp.tile([P, NCH], F32, name="o")
+                outs[(j, mi)] = o
+            o = outs[(j, mi)]
+            nc.vector.tensor_tensor(
+                out=o[:, 4 * r0:4 * r1].rearrange("p (r a) -> p r a", a=4),
+                in0=accs[(j, mi)][:].rearrange("p (a r) -> p r a", a=4)[:, r0:r1, :],
+                in1=bias[:, b0 + 4 * r0:b0 + 4 * r1].rearrange("p (r a) -> p r a", a=4),
+                op=ALU.add,
+            )
+
+        def finish(j, mi, r0, r1):
+            c, j0, func, out_ap, col0 = chunks[j // 2]
+            m = 2 * (j % 2) + mi
+            o = outs[(j, mi)]
+            nc.scalar.activation(out=o[:, 4 * r0:4 * r1], in_=o[:, 4 * r0:4 * r1], func=func)
+            nc.sync.dma_start(out=out_ap.rearrange("(p a) c j -> p a c j", a=4)[:, m, c, col0 + 4 * r0:col0 + 4 * r1], in_=o[:, 4 * r0:4 * r1])
+
+        n_halves = 2 * n_chunks
+        widen(0)
+        for s in range(n_halves + LAG + 1):
+            j = s - LAG
+            if s < n_units:
+                transposes(s)
+            if s % 2 == 1 and 3 <= s <= 11:
+                load_wx_whole((s + 3) // 2)
+                load_bias((s - 1) // 2)
+                if s < 11:
+                    load_wh((s + 5) // 2, 1)
+            if s == 13 or s == 15:
+                load_bias((s - 1) // 2)
+            if 1 <= s <= n_units:
+                quant(s - 1, 1)
+            if 0 <= j - 1 < n_halves - 1:
+                add_bias(j - 1, 1, 0, P)
+            if s < n_units:
+                copy_out(s, 0)
+                copy_out(s, 1)
+            if s == 0:
+                widen(1)
+            if 2 <= s < n_halves:
+                widen(s)
+            if s < n_units:
+                quant(s, 0)
+                copy_out(s, 2)
+                copy_out(s, 3)
+            if 0 <= j - 1 < n_halves:
+                finish(j - 1, 0, 0, P)
+            if 0 <= j - 1 < n_halves - 1:
+                finish(j - 1, 1, 0, P)
+            if j - 1 == n_halves - 1:
+                for r0 in (0, P // 2):
+                    add_bias(j - 1, 1, r0, r0 + P // 2)
+                    finish(j - 1, 1, r0, r0 + P // 2)
+            if 0 <= j < n_halves:
+                matmuls(j)
+                add_bias(j, 0, 0, P)

@@ -45,7 +45,8 @@ def tile_compute_gate_kernel(tc, input_word, hidden_states, Wx_bytes, Wx_scale, 
         ctx.enter_context(tc.manual_schedule())
 
         scale2 = const.tile([P, 2, K], F32, name="scale2")
-        nc.scalar.dma_start(out=scale2[:, 0, :], in_=Wx_scale.rearrange("a b k -> (a b k)").partition_broadcast(P))
+        sc_col = const.tile([P, K // P], F32, name="sc_col")
+        nc.scalar.dma_start(out=sc_col[:], in_=Wx_scale.rearrange("a b (n j) -> n (a b j)", j=K // P))
 
         wxq = []
         wh_raw = []
@@ -104,7 +105,24 @@ def tile_compute_gate_kernel(tc, input_word, hidden_states, Wx_bytes, Wx_scale, 
         junk = const.tile([P, 8], F32, name="junk")
         nc.vector.memset(junk[:], 0.0)
         nc.scalar.activation(out=junk[:, 0:1], in_=junk[:, 0:1], func=ACT.Sigmoid)
-        nc.scalar.copy(out=scale2[:, 1, :], in_=scale2[:, 0, :])
+        sbank = []
+        for hb in range(2):
+            sb_t = psum.tile([P, 4, P], F32, name="acc%d" % hb, tag="acc%d" % hb)
+            sbank.append(sb_t)
+            for jl in range(4):
+                j8 = 4 * hb + jl
+                nc.tensor.transpose(sb_t[:, jl, :], sc_col[:, j8:j8 + 1].to_broadcast([P, P]), ident[:])
+
+        def scale_out(eng_copy, row, hb):
+            eng_copy(
+                out=scale2[:, row, :].rearrange("p (n j) -> p n j", j=K // P)[:, :, 4 * hb:4 * hb + 4],
+                in_=sbank[hb][:].rearrange("p j n -> p n j"),
+            )
+
+        scale_out(nc.vector.tensor_copy, 0, 0)
+        scale_out(nc.scalar.copy, 1, 1)
+        scale_out(nc.vector.tensor_copy, 0, 1)
+        scale_out(nc.scalar.copy, 1, 0)
 
         a_codes = const.tile([P, 4, B], U32, name="a_codes", align_bytes=64)
         a_scl = const.tile([P, 4, B], U8, name="a_scl", align_bytes=64)

@@ -46,7 +46,7 @@ def tile_compute_gate_kernel(tc, input_word, hidden_states, Wx_bytes, Wx_scale, 
 
         scale2 = const.tile([P, 2, K], F32, name="scale2")
         sc_col = const.tile([P, K // P], F32, name="sc_col")
-        nc.scalar.dma_start(out=sc_col[:], in_=Wx_scale.rearrange("a b (n j) -> n (a b j)", j=K // P))
+        nc.scalar.dma_start(out=sc_col[:].rearrange("n (h j) -> n h j", j=4), in_=Wx_scale.rearrange("a b (h n j) -> n (a b h) j", h=2, j=4))
 
         wxq = []
         wh_raw = []
@@ -115,14 +115,14 @@ def tile_compute_gate_kernel(tc, input_word, hidden_states, Wx_bytes, Wx_scale, 
 
         def scale_out(eng_copy, row, hb):
             eng_copy(
-                out=scale2[:, row, :].rearrange("p (n j) -> p n j", j=K // P)[:, :, 4 * hb:4 * hb + 4],
+                out=scale2[:, row, 512 * hb:512 * (hb + 1)].rearrange("p (n j) -> p n j", j=4),
                 in_=sbank[hb][:].rearrange("p j n -> p n j"),
             )
 
         scale_out(nc.vector.tensor_copy, 0, 0)
-        scale_out(nc.scalar.copy, 1, 1)
-        scale_out(nc.vector.tensor_copy, 0, 1)
+        scale_out(nc.scalar.copy, 0, 1)
         scale_out(nc.scalar.copy, 1, 0)
+        scale_out(nc.scalar.copy, 1, 1)
 
         a_codes = const.tile([P, 4, B], U32, name="a_codes", align_bytes=64)
         a_scl = const.tile([P, 4, B], U8, name="a_scl", align_bytes=64)
@@ -141,8 +141,10 @@ def tile_compute_gate_kernel(tc, input_word, hidden_states, Wx_bytes, Wx_scale, 
                 wxb_n = wide.tile([P, 4, K], BF16, name="wxb")
                 wxb[n] = wxb_n
             if w == 0:
-                for a in range(2):
-                    nc.vector.tensor_tensor(out=wxb[n][:, a, :], in0=wxq[n][:, a, :].bitcast(FP8), in1=scale2[:, 0, :], op=ALU.mult)
+                for hb in range(2):
+                    for a in range(2):
+                        ks = slice(512 * hb, 512 * (hb + 1))
+                        nc.vector.tensor_tensor(out=wxb[n][:, a, ks], in0=wxq[n][:, a, ks].bitcast(FP8), in1=scale2[:, 0, ks], op=ALU.mult)
             else:
                 nc.vector.tensor_tensor(
                     out=wxb[n][:, 2 * ap:2 * ap + 2, :].rearrange("p a k -> p (a k)"),
@@ -262,8 +264,11 @@ def tile_compute_gate_kernel(tc, input_word, hidden_states, Wx_bytes, Wx_scale, 
                 copy_out(s, 1)
             if s == 0:
                 widen(1)
-            if 2 <= s < n_halves:
+            if s == 2 or s == 3:
                 widen(s)
+            for w in range(4, n_halves):
+                if min(w + 2, n_halves - 1) == s:
+                    widen(w)
             if s < n_units:
                 quant(s, 0)
                 copy_out(s, 2)

from contextlib import ExitStack

import concourse.mybir as mybir
from concourse.masks import make_identity

F32 = mybir.dt.float32
BF16 = mybir.dt.bfloat16
U32 = mybir.dt.uint32
U8 = mybir.dt.uint8
FP8 = mybir.dt.float8_e4m3fn
FP8X4 = mybir.dt.float8_e4m3fn_x4
ACT = mybir.ActivationFunctionType
ALU = mybir.AluOpType

P = 128
B = 512
K = 1024
H = 1024
C = 2
NCH = 512
FLOPS = 2 * B * (C * 2 * H) * (2 * K)
LAG = 5


def tile_compute_gate_kernel(tc, input_word, hidden_states, Wx_bytes, Wx_scale, bx, Wh, out_0, out_1):
    nc = tc.nc

    chunks = []
    for c in range(C):
        for hf in range(2):
            chunks.append((c, hf * NCH, ACT.Sigmoid, out_1, hf * NCH))
    for c in range(C):
        for hf in range(2):
            chunks.append((c, H + hf * NCH, ACT.Tanh, out_0, hf * NCH))
    n_chunks = len(chunks)

    with ExitStack() as ctx:
        const = ctx.enter_context(tc.tile_pool(name="const", bufs=1))
        raw = ctx.enter_context(tc.tile_pool(name="raw", bufs=1))
        wide = ctx.enter_context(tc.tile_pool(name="wide", bufs=3))
        grpp = ctx.enter_context(tc.tile_pool(name="grpp", bufs=4))
        codep = ctx.enter_context(tc.tile_pool(name="codep", bufs=3))
        outp = ctx.enter_context(tc.tile_pool(name="outp", bufs=6))
        psum = ctx.enter_context(tc.psum_pool(name="psum", bufs=1))
        ctx.enter_context(tc.manual_schedule())

        scale2 = const.tile([P, 2, K], F32, name="scale2")
        sc_col = const.tile([P, K // P], F32, name="sc_col")
        nc.scalar.dma_start(out=sc_col[:].rearrange("n (h j) -> n h j", j=4), in_=Wx_scale.rearrange("a b (h n j) -> n (a b h) j", h=2, j=4))

        wxq = []
        wh_raw = []
        for n in range(n_chunks):
            wxq_n = raw.tile([P, 4, K], U8, name="wxq%d" % n, tag="wxq%d" % n)
            wxq.append(wxq_n)
            wh_n = raw.tile([P, 4, K], BF16, name="whr%d" % n, tag="whr%d" % n)
            wh_raw.append(wh_n)
        h_raw = raw.tile([P, 4, K], BF16, name="h_raw")
        x_raw = raw.tile([P, 4, K], BF16, name="x_raw")
        bias = const.tile([P, C * 2 * H], BF16, name="bias")

        def load_wx(n, parts):
            c, j0 = chunks[n][0], chunks[n][1]
            src = Wx_bytes[c, j0:j0 + NCH, :].rearrange("(p a) k -> p a k", a=4)
            for i in parts:
                nc.sync.dma_start(out=wxq[n][:, 2 * i:2 * i + 2, :], in_=src[:, 2 * i:2 * i + 2, :])

        def load_wx_whole(n):
            c, j0 = chunks[n][0], chunks[n][1]
            nc.sync.dma_start(out=wxq[n][:], in_=Wx_bytes[c, j0:j0 + NCH, :].rearrange("(p a) k -> p a k", a=4))

        def load_bias(n):
            c, j0 = chunks[n][0], chunks[n][1]
            b0 = c * 2 * H + j0
            nc.sync.dma_start(out=bias[:, b0:b0 + NCH], in_=bx[c, j0:j0 + NCH].partition_broadcast(P))

        def load_wh(n, parts):
            c, j0 = chunks[n][0], chunks[n][1]
            src = Wh[c, j0:j0 + NCH, :].rearrange("(p a) k -> p a k", a=4)
            step = 4 // parts
            for i in range(parts):
                nc.sync.dma_start(out=wh_raw[n][:, i * step:(i + 1) * step, :], in_=src[:, i * step:(i + 1) * step, :])

        def load_act(dst, src_ap, a0, a1):
            src = src_ap.rearrange("(p a) k -> p a k", a=4)
            nc.sync.dma_start(out=dst[:, a0:a1, :], in_=src[:, a0:a1, :])

        load_act(h_raw, hidden_states, 0, 1)
        load_wx(0, [0])
        load_act(h_raw, hidden_states, 1, 2)
        load_act(h_raw, hidden_states, 2, 4)
        load_wx(0, [1])
        load_act(x_raw, input_word, 0, 2)
        load_act(x_raw, input_word, 2, 4)
        load_wh(0, 2)
        load_wx_whole(1)
        load_wh(1, 1)
        load_wh(2, 1)
        load_wx_whole(2)
        load_bias(0)
        load_wh(3, 1)

        ident = const.tile([P, P], F32, name="ident")
        make_identity(nc, ident[:])
        junk = const.tile([P, 8], F32, name="junk")
        nc.vector.memset(junk[:], 0.0)
        nc.scalar.activation(out=junk[:, 0:1], in_=junk[:, 0:1], func=ACT.Sigmoid)
        sbank = []
        for hb in range(2):
            sb_t = psum.tile([P, 4, P], F32, name="acc%d" % hb, tag="acc%d" % hb)
            sbank.append(sb_t)
            for jl in range(4):
                j8 = 4 * hb + jl
                nc.tensor.transpose(sb_t[:, jl, :], sc_col[:, j8:j8 + 1].to_broadcast([P, P]), ident[:])

        def scale_out(eng_copy, row, hb):
            eng_copy(
                out=scale2[:, row, 512 * hb:512 * (hb + 1)].rearrange("p (n j) -> p n j", j=4),
                in_=sbank[hb][:].rearrange("p j n -> p n j"),
            )

        scale_out(nc.vector.tensor_copy, 0, 0)
        scale_out(nc.scalar.copy, 0, 1)
        scale_out(nc.scalar.copy, 1, 0)
        scale_out(nc.scalar.copy, 1, 1)

        a_codes = const.tile([P, 4, B], U32, name="a_codes", align_bytes=64)
        a_scl = const.tile([P, 4, B], U8, name="a_scl", align_bytes=64)

        wxb = {}
        w_codes = {}
        w_scl = {}
        banks = {}
        grps = {}
        accs = {}
        outs = {}

        def widen(w):
            n, ap = w // 2, w % 2
            if ap == 0:
                wxb_n = wide.tile([P, 4, K], BF16, name="wxb")
                wxb[n] = wxb_n
            if w == 0:
                for hb in range(2):
                    for a in range(2):
                        ks = slice(512 * hb, 512 * (hb + 1))
                        nc.vector.tensor_tensor(out=wxb[n][:, a, ks], in0=wxq[n][:, a, ks].bitcast(FP8), in1=scale2[:, 0, ks], op=ALU.mult)
            else:
                nc.vector.tensor_tensor(
                    out=wxb[n][:, 2 * ap:2 * ap + 2, :].rearrange("p a k -> p (a k)"),
                    in0=wxq[n][:, 2 * ap:2 * ap + 2, :].rearrange("p a k -> p (a k)").bitcast(FP8),
                    in1=scale2[:].rearrange("p a k -> p (a k)"),
                    op=ALU.mult,
                )

        seq = [("act", h_raw, 0), ("act", x_raw, 2), ("w", 0, 0), ("w", 0, 2), ("w", 1, 0)]
        for n in range(1, n_chunks - 1):
            seq.append(("w", n + 1, 0))
            seq.append(("w", n, 2))
        seq.append(("w", n_chunks - 1, 2))
        n_units = len(seq)

        def unit_src(s):
            kind, what, ps0 = seq[s]
            if kind == "act":
                return what
            return wh_raw[what] if ps0 == 0 else wxb[what]

        def transposes(s):
            src = unit_src(s)
            for g in range(2):
                for ap in range(2):
                    b = 2 * g + ap
                    tp = psum.tile([P, 2, 256], F32, name="tp%d" % b, tag="tp%d" % b)
                    banks[(s, b)] = tp
                    for al in range(2):
                        words = src[:, 2 * ap + al, :].bitcast(F32)
                        for u in range(2):
                            nc.tensor.transpose(tp[:, u, al * P:(al + 1) * P], words[:, 256 * g + u:256 * (g + 1):2], ident[:])

        def copy_out(s, b):
            g, ap = b // 2, b % 2
            if ap == 0:
                grp = grpp.tile([P, NCH, 4], BF16, name="grp", align_bytes=64)
                grps[(s, g)] = grp
            grp = grps[(s, g)]
            dst = grp[:, ap * 256:(ap + 1) * 256, :].rearrange("p c t -> p (c t)").bitcast(F32).rearrange("p (c u) -> p c u", u=2)
            nc.scalar.copy(out=dst, in_=banks[(s, b)][:].rearrange("p u c -> p c u"))

        def quant(s, g):
            kind, what, ps0 = seq[s]
            if kind == "act":
                cod, scl = a_codes, a_scl
            else:
                if ps0 == 0 and g == 0:
                    wc = codep.tile([P, 4, NCH], U32, name="wc", align_bytes=64)
                    ws = codep.tile([P, 4, NCH], U8, name="ws", align_bytes=64)
                    w_codes[what] = wc
                    w_scl[what] = ws
                cod, scl = w_codes[what], w_scl[what]
            nc.vector.quantize_mx(
                out=cod[:, ps0 + g, :].bitcast(FP8X4),
                scales=scl[:, ps0 + g, :],
                in_=grps[(s, g)][:].rearrange("p c t -> p (c t)"),
            )

        def matmuls(j):
            n = j // 2
            for mi in range(2):
                m = 2 * (j % 2) + mi
                acc = psum.tile([P, NCH], F32, name="acc%d" % m, tag="acc%d" % m)
                accs[(j, mi)] = acc
                for ps in range(4):
                    nc.tensor.matmul_mx(
                        out=acc[:],
                        lhsT=a_codes[:, ps, m * P:(m + 1) * P].bitcast(FP8X4),
                        lhsT_scale=a_scl[:, ps, m * P:(m + 1) * P],
                        rhs=w_codes[n][:, ps, :].bitcast(FP8X4),
                        rhs_scale=w_scl[n][:, ps, :],
                        start=(ps == 0),
                        stop=(ps == 3),
                    )

        def add_bias(j, mi, r0, r1):
            c, j0 = chunks[j // 2][0], chunks[j // 2][1]
            b0 = c * 2 * H + j0
            if r0 == 0:
                o = outp.tile([P, NCH], F32, name="o")
                outs[(j, mi)] = o
            o = outs[(j, mi)]
            nc.vector.tensor_tensor(
                out=o[:, 4 * r0:4 * r1].rearrange("p (r a) -> p r a", a=4),
                in0=accs[(j, mi)][:].rearrange("p (a r) -> p r a", a=4)[:, r0:r1, :],
                in1=bias[:, b0 + 4 * r0:b0 + 4 * r1].rearrange("p (r a) -> p r a", a=4),
                op=ALU.add,
            )

        def finish(j, mi, r0, r1):
            c, j0, func, out_ap, col0 = chunks[j // 2]
            m = 2 * (j % 2) + mi
            o = outs[(j, mi)]
            nc.scalar.activation(out=o[:, 4 * r0:4 * r1], in_=o[:, 4 * r0:4 * r1], func=func)
            nc.sync.dma_start(out=out_ap.rearrange("(p a) c j -> p a c j", a=4)[:, m, c, col0 + 4 * r0:col0 + 4 * r1], in_=o[:, 4 * r0:4 * r1])

        n_halves = 2 * n_chunks
        widen(0)
        for s in range(n_halves + LAG + 1):
            j = s - LAG
            if s < n_units:
                transposes(s)
            if s % 2 == 1 and 3 <= s <= 11:
                load_wx_whole((s + 3) // 2)
                load_bias((s - 1) // 2)
                if s < 11:
                    load_wh((s + 5) // 2, 1)
            if s == 13 or s == 15:
                load_bias((s - 1) // 2)
            if 1 <= s <= n_units:
                quant(s - 1, 1)
            if 0 <= j - 1 < n_halves - 1:
                add_bias(j - 1, 1, 0, P)
            if s < n_units:
                copy_out(s, 0)
                copy_out(s, 1)
            if s == 0:
                widen(1)
            if s == 2 or s == 3:
                widen(s)
            for w in range(4, n_halves):
                if min(w + 2, n_halves - 1) == s:
                    widen(w)
            if s < n_units:
                quant(s, 0)
                copy_out(s, 2)
                copy_out(s, 3)
            if 0 <= j - 1 < n_halves:
                finish(j - 1, 0, 0, P)
            if 0 <= j - 1 < n_halves - 1:
                finish(j - 1, 1, 0, P)
            if j - 1 == n_halves - 1:
                for r0 in (0, P // 2):
                    add_bias(j - 1, 1, r0, r0 + P // 2)
                    finish(j - 1, 1, r0, r0 + P // 2)
            if 0 <= j < n_halves:
                matmuls(j)
                add_bias(j, 0, 0, P)
